import numpy as np
import ml_dtypes

BF16 = ml_dtypes.bfloat16


def bf(x):
    return np.asarray(x, np.float32).astype(BF16)


def f32(x):
    return np.asarray(x, np.float32)


def f64(x):
    return np.asarray(x).astype(np.float64)


def striped(idx):
    return np.tile(idx.reshape(-1, 16).T, (8, 1))


C, V, S, N = 128, 256, 256, 128
ETA = 0.1
BETA = 0.1
ITER_N = 3
RHO = 1.0 / float((ITER_N + 5) ** 0.9)
E_SCALE = 0.1
BOW_MEAN = 1.0


def setup_inputs():
    return {"x": f32(np.random.random((C, S))), "exp_n": f32(E_SCALE * np.random.standard_exponential((C, V)) ** 2), "bow": f32(np.random.poisson(BOW_MEAN, (V, N))), "offs": striped(np.random.permutation(S)[:N])}


def reference(x, exp_n, bow, offs):
    idx = offs[:16].T.reshape(-1)
    picked = f64(x)[:, idx]
    theta = picked + ETA
    e = f64(exp_n)
    reg = (BETA + e) / (BETA * V + e.sum(axis=1, keepdims=True))
    r = reg.T @ theta
    q = f64(bow) / r
    u = reg @ q
    return (1.0 - RHO) * picked + RHO * theta * u

@@ -1,0 +1,78 @@
+import concourse.mybir as mybir
+from concourse.masks import make_identity
+
+F32, BF16, U16 = mybir.dt.float32, mybir.dt.bfloat16, mybir.dt.uint16
+ADD, MULT = mybir.AluOpType.add, mybir.AluOpType.mult
+
+P = 128
+C, V, S, N = 128, 256, 256, 128
+VB = V // P
+ETA = 0.1
+BETA = 0.1
+RHO = 8.0 ** (-0.9)
+
+FLOPS = 2 * 2 * C * V * N
+
+
+def tile_mixehr_seed_kernel(tc, x, exp_n, bow, offs, out):
+    nc = tc.nc
+    with (
+        tc.tile_pool(name="held", bufs=1) as held,
+        tc.psum_pool(name="psum", bufs=1) as psum,
+    ):
+        offsets = held.tile([P, N // 16], U16, name="offsets")
+        nc.sync.dma_start(offsets[:], offs)
+        docs = held.tile([C, S], F32, name="docs")
+        nc.sync.dma_start(docs[:], x)
+        counts = held.tile([C, V], F32, name="counts")
+        nc.scalar.dma_start(counts[:], exp_n)
+        words = held.tile([P, VB, N], F32, name="words")
+        nc.scalar.dma_start(words[:], bow.rearrange("(b p) j -> p b j", p=P))
+
+        eta = held.tile([C, N], F32, name="eta")
+        nc.gpsimd.memset(eta[:], ETA)
+        ident = held.tile([P, P], BF16, name="ident")
+        make_identity(nc, ident[:])
+
+        theta = held.tile([C, N], F32, name="theta")
+        nc.vector.tensor_tensor(theta[:], docs[:].indirect(offsets[:]), eta[:], ADD)
+        theta_bf = held.tile([C, N], BF16, name="theta_bf")
+        nc.gpsimd.tensor_copy(theta_bf[:], theta[:])
+
+        fresh = held.tile([C, N], F32, name="fresh")
+        nc.gpsimd.tensor_scalar_mul(fresh[:], theta[:], RHO)
+        kept = held.tile([C, N], F32, name="kept")
+        nc.gpsimd.tensor_scalar(kept[:], theta[:], -ETA, 1.0 - RHO, op0=ADD, op1=MULT)
+
+        smoothed = held.tile([C, V], F32, name="smoothed")
+        nc.vector.tensor_scalar_add(smoothed[:], counts[:], BETA)
+        total = held.tile([C, 1], F32, name="total")
+        nc.vector.reduce_sum(total[:], smoothed[:], axis=mybir.AxisListType.X)
+        share = held.tile([C, 1], F32, name="share")
+        nc.vector.reciprocal(share[:], total[:])
+        reg_bf = held.tile([C, V], BF16, name="reg_bf")
+        nc.vector.tensor_scalar_mul(reg_bf[:], smoothed[:], share[:, 0:1])
+
+        r = psum.tile([P, VB, N], F32, name="r")
+        for b in range(VB):
+            nc.tensor.matmul(r[:, b, :], lhsT=reg_bf[:, b * P : (b + 1) * P], rhs=theta_bf[:], start=True, stop=True)
+
+        reg_t_ps = psum.tile([P, VB, C], BF16, name="reg_t_ps")
+        for b in range(VB):
+            nc.tensor.transpose(reg_t_ps[:, b, :], reg_bf[:, b * P : (b + 1) * P], ident[:])
+        reg_t = held.tile([P, VB, C], BF16, name="reg_t")
+        nc.scalar.copy(reg_t[:], reg_t_ps[:])
+
+        r_inv = held.tile([P, VB, N], F32, name="r_inv")
+        nc.vector.reciprocal(r_inv[:], r[:])
+        q_bf = held.tile([P, VB, N], BF16, name="q_bf")
+        nc.vector.tensor_tensor(q_bf[:], r_inv[:], words[:], MULT)
+
+        u = psum.tile([C, N], F32, name="u")
+        for b in range(VB):
+            nc.tensor.matmul(u[:], lhsT=reg_t[:, b, :], rhs=q_bf[:, b, :], start=(b == 0), stop=(b == VB - 1))
+
+        result = held.tile([C, N], F32, name="result")
+        nc.vector.tensor_tensor(result[:], u[:], fresh[:], MULT)
+        nc.vector.tensor_tensor(result[:], result[:], kept[:], ADD)
+        nc.sync.dma_start(out, result[:])

@@ -3,6 +3,7 @@ from concourse.masks import make_identity
 
 F32, BF16, U16 = mybir.dt.float32, mybir.dt.bfloat16, mybir.dt.uint16
 ADD, MULT = mybir.AluOpType.add, mybir.AluOpType.mult
+IDENTITY = mybir.ActivationFunctionType.Identity
 
 P = 128
 C, V, S, N = 128, 256, 256, 128
@@ -31,6 +32,8 @@ def tile_mixehr_seed_kernel(tc, x, exp_n, bow, offs, out):
 
         eta = held.tile([C, N], F32, name="eta")
         nc.gpsimd.memset(eta[:], ETA)
+        beta = held.tile([C, 1], F32, name="beta")
+        nc.gpsimd.memset(beta[:], BETA)
         ident = held.tile([P, P], BF16, name="ident")
         make_identity(nc, ident[:])
 
@@ -45,9 +48,8 @@ def tile_mixehr_seed_kernel(tc, x, exp_n, bow, offs, out):
         nc.gpsimd.tensor_scalar(kept[:], theta[:], -ETA, 1.0 - RHO, op0=ADD, op1=MULT)
 
         smoothed = held.tile([C, V], F32, name="smoothed")
-        nc.vector.tensor_scalar_add(smoothed[:], counts[:], BETA)
         total = held.tile([C, 1], F32, name="total")
-        nc.vector.reduce_sum(total[:], smoothed[:], axis=mybir.AxisListType.X)
+        nc.scalar.activation(smoothed[:], counts[:], IDENTITY, bias=beta[:, 0:1], accum_out=total[:])
         share = held.tile([C, 1], F32, name="share")
         nc.vector.reciprocal(share[:], total[:])
         reg_bf = held.tile([C, V], BF16, name="reg_bf")

@@ -34,6 +34,8 @@ def tile_mixehr_seed_kernel(tc, x, exp_n, bow, offs, out):
         nc.gpsimd.memset(eta[:], ETA)
         beta = held.tile([C, 1], F32, name="beta")
         nc.gpsimd.memset(beta[:], BETA)
+        warm = held.tile([C, 1], F32, name="warm")
+        nc.scalar.activation(warm[:], beta[:], IDENTITY)
         ident = held.tile([P, P], BF16, name="ident")
         make_identity(nc, ident[:])
 

@@ -8,6 +8,7 @@ IDENTITY = mybir.ActivationFunctionType.Identity
 P = 128
 C, V, S, N = 128, 256, 256, 128
 VB = V // P
+HALF = N // 2
 ETA = 0.1
 BETA = 0.1
 RHO = 8.0 ** (-0.9)
@@ -28,7 +29,7 @@ def tile_mixehr_seed_kernel(tc, x, exp_n, bow, offs, out):
         counts = held.tile([C, V], F32, name="counts")
         nc.scalar.dma_start(counts[:], exp_n)
         words = held.tile([P, VB, N], F32, name="words")
-        nc.scalar.dma_start(words[:], bow.rearrange("(b p) j -> p b j", p=P))
+        nc.sync.dma_start(words[:], bow.rearrange("(b p) j -> p b j", p=P))
 
         eta = held.tile([C, N], F32, name="eta")
         nc.gpsimd.memset(eta[:], ETA)
@@ -42,7 +43,7 @@ def tile_mixehr_seed_kernel(tc, x, exp_n, bow, offs, out):
         theta = held.tile([C, N], F32, name="theta")
         nc.vector.tensor_tensor(theta[:], docs[:].indirect(offsets[:]), eta[:], ADD)
         theta_bf = held.tile([C, N], BF16, name="theta_bf")
-        nc.gpsimd.tensor_copy(theta_bf[:], theta[:])
+        nc.vector.tensor_copy(theta_bf[:], theta[:])
 
         fresh = held.tile([C, N], F32, name="fresh")
         nc.gpsimd.tensor_scalar_mul(fresh[:], theta[:], RHO)
@@ -67,16 +68,21 @@ def tile_mixehr_seed_kernel(tc, x, exp_n, bow, offs, out):
         reg_t = held.tile([P, VB, C], BF16, name="reg_t")
         nc.scalar.copy(reg_t[:], reg_t_ps[:])
 
-        r_inv = held.tile([P, VB, N], F32, name="r_inv")
-        nc.vector.reciprocal(r_inv[:], r[:])
-        q_bf = held.tile([P, VB, N], BF16, name="q_bf")
-        nc.vector.tensor_tensor(q_bf[:], r_inv[:], words[:], MULT)
+        halves = [slice(h * HALF, (h + 1) * HALF) for h in range(2)]
+        multipliers = [nc.gpsimd, nc.vector]
+        q_bf = []
+        for h, (half, multiplier) in enumerate(zip(halves, multipliers)):
+            r_inv = held.tile([P, VB, HALF], F32, name=f"r_inv{h}")
+            nc.vector.reciprocal(r_inv[:], r[:, :, half])
+            q_bf.append(held.tile([P, VB, HALF], BF16, name=f"q_bf{h}"))
+            multiplier.tensor_tensor(q_bf[h][:], r_inv[:], words[:, :, half], MULT)
 
-        u = psum.tile([C, N], F32, name="u")
-        for b in range(VB):
-            nc.tensor.matmul(u[:], lhsT=reg_t[:, b, :], rhs=q_bf[:, b, :], start=(b == 0), stop=(b == VB - 1))
-
-        result = held.tile([C, N], F32, name="result")
-        nc.vector.tensor_tensor(result[:], u[:], fresh[:], MULT)
-        nc.vector.tensor_tensor(result[:], result[:], kept[:], ADD)
-        nc.sync.dma_start(out, result[:])
+        stores = [nc.scalar, nc.sync]
+        for h, (half, store) in enumerate(zip(halves, stores)):
+            u = psum.tile([C, HALF], F32, name=f"u{h}")
+            for b in range(VB):
+                nc.tensor.matmul(u[:], lhsT=reg_t[:, b, :], rhs=q_bf[h][:, b, :], start=(b == 0), stop=(b == VB - 1))
+            result = held.tile([C, HALF], F32, name=f"result{h}")
+            nc.vector.tensor_tensor(result[:], u[:], fresh[:, half], MULT)
+            nc.vector.tensor_tensor(result[:], result[:], kept[:, half], ADD)
+            store.dma_start(out[:, half], result[:])

@@ -4,11 +4,14 @@ from concourse.masks import make_identity
 F32, BF16, U16 = mybir.dt.float32, mybir.dt.bfloat16, mybir.dt.uint16
 ADD, MULT = mybir.AluOpType.add, mybir.AluOpType.mult
 IDENTITY = mybir.ActivationFunctionType.Identity
+SIGN = mybir.ActivationFunctionType.Sign
+SQUARE = mybir.ActivationFunctionType.Square
+ABS_RSQRT = mybir.ActivationFunctionType.Abs_reciprocal_sqrt
 
 P = 128
 C, V, S, N = 128, 256, 256, 128
 VB = V // P
-HALF = N // 2
+VECTOR_DOCS = 64
 ETA = 0.1
 BETA = 0.1
 RHO = 8.0 ** (-0.9)
@@ -36,7 +39,7 @@ def tile_mixehr_seed_kernel(tc, x, exp_n, bow, offs, out):
         beta = held.tile([C, 1], F32, name="beta")
         nc.gpsimd.memset(beta[:], BETA)
         warm = held.tile([C, 1], F32, name="warm")
-        nc.scalar.activation(warm[:], beta[:], IDENTITY)
+        nc.scalar.activation(warm[:], beta[:], ABS_RSQRT)
         ident = held.tile([P, P], BF16, name="ident")
         make_identity(nc, ident[:])
 
@@ -58,31 +61,41 @@ def tile_mixehr_seed_kernel(tc, x, exp_n, bow, offs, out):
         reg_bf = held.tile([C, V], BF16, name="reg_bf")
         nc.vector.tensor_scalar_mul(reg_bf[:], smoothed[:], share[:, 0:1])
 
-        r = psum.tile([P, VB, N], F32, name="r")
-        for b in range(VB):
-            nc.tensor.matmul(r[:, b, :], lhsT=reg_bf[:, b * P : (b + 1) * P], rhs=theta_bf[:], start=True, stop=True)
+        parts = [slice(0, VECTOR_DOCS), slice(VECTOR_DOCS, N)]
+        widths = [VECTOR_DOCS, N - VECTOR_DOCS]
+        r = [psum.tile([P, VB, width], F32, name=f"r{k}") for k, width in enumerate(widths)]
+        for k, part in enumerate(parts):
+            for b in range(VB):
+                nc.tensor.matmul(
+                    r[k][:, b, :], lhsT=reg_bf[:, b * P : (b + 1) * P], rhs=theta_bf[:, part], start=True, stop=True
+                )
 
         reg_t_ps = psum.tile([P, VB, C], BF16, name="reg_t_ps")
         for b in range(VB):
             nc.tensor.transpose(reg_t_ps[:, b, :], reg_bf[:, b * P : (b + 1) * P], ident[:])
         reg_t = held.tile([P, VB, C], BF16, name="reg_t")
+
+        q_bf = [held.tile([P, VB, width], BF16, name=f"q_bf{k}") for k, width in enumerate(widths)]
+        r_inv = held.tile([P, VB, widths[0]], F32, name="r_inv")
+        nc.vector.reciprocal(r_inv[:], r[0][:])
+        nc.vector.tensor_tensor(q_bf[0][:], r_inv[:], words[:, :, parts[0]], MULT)
+        r_sign = held.tile([P, VB, widths[1]], F32, name="r_sign")
+        nc.scalar.activation(r_sign[:], r[1][:], SIGN)
+        signed_words = held.tile([P, VB, widths[1]], F32, name="signed_words")
+        nc.gpsimd.tensor_tensor(signed_words[:], r_sign[:], words[:, :, parts[1]], MULT)
+        r_root = held.tile([P, VB, widths[1]], F32, name="r_root")
+        nc.scalar.activation(r_root[:], r[1][:], ABS_RSQRT)
+        r_size = held.tile([P, VB, widths[1]], F32, name="r_size")
+        nc.scalar.activation(r_size[:], r_root[:], SQUARE)
+        nc.vector.tensor_tensor(q_bf[1][:], r_size[:], signed_words[:], MULT)
         nc.scalar.copy(reg_t[:], reg_t_ps[:])
 
-        halves = [slice(h * HALF, (h + 1) * HALF) for h in range(2)]
-        multipliers = [nc.gpsimd, nc.vector]
-        q_bf = []
-        for h, (half, multiplier) in enumerate(zip(halves, multipliers)):
-            r_inv = held.tile([P, VB, HALF], F32, name=f"r_inv{h}")
-            nc.vector.reciprocal(r_inv[:], r[:, :, half])
-            q_bf.append(held.tile([P, VB, HALF], BF16, name=f"q_bf{h}"))
-            multiplier.tensor_tensor(q_bf[h][:], r_inv[:], words[:, :, half], MULT)
-
         stores = [nc.scalar, nc.sync]
-        for h, (half, store) in enumerate(zip(halves, stores)):
-            u = psum.tile([C, HALF], F32, name=f"u{h}")
+        for k, (part, store) in enumerate(zip(parts, stores)):
+            u = psum.tile([C, widths[k]], F32, name=f"u{k}")
             for b in range(VB):
-                nc.tensor.matmul(u[:], lhsT=reg_t[:, b, :], rhs=q_bf[h][:, b, :], start=(b == 0), stop=(b == VB - 1))
-            result = held.tile([C, HALF], F32, name=f"result{h}")
-            nc.vector.tensor_tensor(result[:], u[:], fresh[:, half], MULT)
-            nc.vector.tensor_tensor(result[:], result[:], kept[:, half], ADD)
-            store.dma_start(out[:, half], result[:])
+                nc.tensor.matmul(u[:], lhsT=reg_t[:, b, :], rhs=q_bf[k][:, b, :], start=(b == 0), stop=(b == VB - 1))
+            result = held.tile([C, widths[k]], F32, name=f"result{k}")
+            nc.vector.tensor_tensor(result[:], u[:], fresh[:, part], MULT)
+            nc.vector.tensor_tensor(result[:], result[:], kept[:, part], ADD)
+            store.dma_start(out[:, part], result[:])

@@ -15,6 +15,8 @@ VECTOR_DOCS = 64
 ETA = 0.1
 BETA = 0.1
 RHO = 8.0 ** (-0.9)
+OLD_TO_NEW = (1.0 - RHO) / RHO
+KEPT_ETA = (1.0 - RHO) * ETA
 
 FLOPS = 2 * 2 * C * V * N
 
@@ -25,10 +27,10 @@ def tile_mixehr_seed_kernel(tc, x, exp_n, bow, offs, out):
         tc.tile_pool(name="held", bufs=1) as held,
         tc.psum_pool(name="psum", bufs=1) as psum,
     ):
-        offsets = held.tile([P, N // 16], U16, name="offsets")
-        nc.sync.dma_start(offsets[:], offs)
         docs = held.tile([C, S], F32, name="docs")
         nc.sync.dma_start(docs[:], x)
+        offsets = held.tile([P, N // 16], U16, name="offsets")
+        nc.sync.dma_start(offsets[:], offs)
         counts = held.tile([C, V], F32, name="counts")
         nc.scalar.dma_start(counts[:], exp_n)
         words = held.tile([P, VB, N], F32, name="words")
@@ -50,8 +52,6 @@ def tile_mixehr_seed_kernel(tc, x, exp_n, bow, offs, out):
 
         fresh = held.tile([C, N], F32, name="fresh")
         nc.gpsimd.tensor_scalar_mul(fresh[:], theta[:], RHO)
-        kept = held.tile([C, N], F32, name="kept")
-        nc.gpsimd.tensor_scalar(kept[:], theta[:], -ETA, 1.0 - RHO, op0=ADD, op1=MULT)
 
         smoothed = held.tile([C, V], F32, name="smoothed")
         total = held.tile([C, 1], F32, name="total")
@@ -96,6 +96,6 @@ def tile_mixehr_seed_kernel(tc, x, exp_n, bow, offs, out):
             for b in range(VB):
                 nc.tensor.matmul(u[:], lhsT=reg_t[:, b, :], rhs=q_bf[k][:, b, :], start=(b == 0), stop=(b == VB - 1))
             result = held.tile([C, widths[k]], F32, name=f"result{k}")
-            nc.vector.tensor_tensor(result[:], u[:], fresh[:, part], MULT)
-            nc.vector.tensor_tensor(result[:], result[:], kept[:, part], ADD)
+            nc.vector.scalar_tensor_tensor(result[:], u[:], OLD_TO_NEW, fresh[:, part], op0=ADD, op1=MULT)
+            nc.vector.tensor_scalar_add(result[:], result[:], -KEPT_ETA)
             store.dma_start(out[:, part], result[:])

@@ -48,7 +48,7 @@ def tile_mixehr_seed_kernel(tc, x, exp_n, bow, offs, out):
         theta = held.tile([C, N], F32, name="theta")
         nc.vector.tensor_tensor(theta[:], docs[:].indirect(offsets[:]), eta[:], ADD)
         theta_bf = held.tile([C, N], BF16, name="theta_bf")
-        nc.vector.tensor_copy(theta_bf[:], theta[:])
+        nc.scalar.copy(theta_bf[:], theta[:])
 
         fresh = held.tile([C, N], F32, name="fresh")
         nc.gpsimd.tensor_scalar_mul(fresh[:], theta[:], RHO)

@@ -50,8 +50,6 @@ def tile_mixehr_seed_kernel(tc, x, exp_n, bow, offs, out):
         theta_bf = held.tile([C, N], BF16, name="theta_bf")
         nc.scalar.copy(theta_bf[:], theta[:])
 
-        fresh = held.tile([C, N], F32, name="fresh")
-        nc.gpsimd.tensor_scalar_mul(fresh[:], theta[:], RHO)
 
         smoothed = held.tile([C, V], F32, name="smoothed")
         total = held.tile([C, 1], F32, name="total")
@@ -96,6 +94,6 @@ def tile_mixehr_seed_kernel(tc, x, exp_n, bow, offs, out):
             for b in range(VB):
                 nc.tensor.matmul(u[:], lhsT=reg_t[:, b, :], rhs=q_bf[k][:, b, :], start=(b == 0), stop=(b == VB - 1))
             result = held.tile([C, widths[k]], F32, name=f"result{k}")
-            nc.vector.scalar_tensor_tensor(result[:], u[:], OLD_TO_NEW, fresh[:, part], op0=ADD, op1=MULT)
-            nc.vector.tensor_scalar_add(result[:], result[:], -KEPT_ETA)
+            nc.vector.scalar_tensor_tensor(result[:], u[:], OLD_TO_NEW, theta[:, part], op0=ADD, op1=MULT)
+            nc.vector.tensor_scalar(result[:], result[:], RHO, -KEPT_ETA, op0=MULT, op1=ADD)
             store.dma_start(out[:, part], result[:])

@@ -11,7 +11,6 @@ ABS_RSQRT = mybir.ActivationFunctionType.Abs_reciprocal_sqrt
 P = 128
 C, V, S, N = 128, 256, 256, 128
 VB = V // P
-VECTOR_DOCS = 64
 ETA = 0.1
 BETA = 0.1
 RHO = 8.0 ** (-0.9)
@@ -50,50 +49,43 @@ def tile_mixehr_seed_kernel(tc, x, exp_n, bow, offs, out):
         theta_bf = held.tile([C, N], BF16, name="theta_bf")
         nc.scalar.copy(theta_bf[:], theta[:])
 
-
         smoothed = held.tile([C, V], F32, name="smoothed")
         total = held.tile([C, 1], F32, name="total")
         nc.scalar.activation(smoothed[:], counts[:], IDENTITY, bias=beta[:, 0:1], accum_out=total[:])
         share = held.tile([C, 1], F32, name="share")
         nc.vector.reciprocal(share[:], total[:])
-        reg_bf = held.tile([C, V], BF16, name="reg_bf")
-        nc.vector.tensor_scalar_mul(reg_bf[:], smoothed[:], share[:, 0:1])
+        reg_bf = [held.tile([C, P], BF16, name=f"reg_bf{b}") for b in range(VB)]
+        for b in range(VB):
+            nc.vector.tensor_scalar_mul(reg_bf[b][:], smoothed[:, b * P : (b + 1) * P], share[:, 0:1])
 
-        parts = [slice(0, VECTOR_DOCS), slice(VECTOR_DOCS, N)]
-        widths = [VECTOR_DOCS, N - VECTOR_DOCS]
-        r = [psum.tile([P, VB, width], F32, name=f"r{k}") for k, width in enumerate(widths)]
-        for k, part in enumerate(parts):
-            for b in range(VB):
-                nc.tensor.matmul(
-                    r[k][:, b, :], lhsT=reg_bf[:, b * P : (b + 1) * P], rhs=theta_bf[:, part], start=True, stop=True
-                )
+        r = [psum.tile([P, N], F32, name=f"r{b}") for b in range(VB)]
+        for b in range(VB):
+            nc.tensor.matmul(r[b][:], lhsT=reg_bf[b][:], rhs=theta_bf[:], start=True, stop=True)
 
         reg_t_ps = psum.tile([P, VB, C], BF16, name="reg_t_ps")
         for b in range(VB):
-            nc.tensor.transpose(reg_t_ps[:, b, :], reg_bf[:, b * P : (b + 1) * P], ident[:])
+            nc.tensor.transpose(reg_t_ps[:, b, :], reg_bf[b][:], ident[:])
         reg_t = held.tile([P, VB, C], BF16, name="reg_t")
 
-        q_bf = [held.tile([P, VB, width], BF16, name=f"q_bf{k}") for k, width in enumerate(widths)]
-        r_inv = held.tile([P, VB, widths[0]], F32, name="r_inv")
+        q_bf = [held.tile([P, N], BF16, name=f"q_bf{b}") for b in range(VB)]
+        r_inv = held.tile([P, N], F32, name="r_inv")
         nc.vector.reciprocal(r_inv[:], r[0][:])
-        nc.vector.tensor_tensor(q_bf[0][:], r_inv[:], words[:, :, parts[0]], MULT)
-        r_sign = held.tile([P, VB, widths[1]], F32, name="r_sign")
+        nc.vector.tensor_tensor(q_bf[0][:], r_inv[:], words[:, 0, :], MULT)
+        r_sign = held.tile([P, N], F32, name="r_sign")
         nc.scalar.activation(r_sign[:], r[1][:], SIGN)
-        signed_words = held.tile([P, VB, widths[1]], F32, name="signed_words")
-        nc.gpsimd.tensor_tensor(signed_words[:], r_sign[:], words[:, :, parts[1]], MULT)
-        r_root = held.tile([P, VB, widths[1]], F32, name="r_root")
+        signed_words = held.tile([P, N], F32, name="signed_words")
+        nc.gpsimd.tensor_tensor(signed_words[:], r_sign[:], words[:, 1, :], MULT)
+        r_root = held.tile([P, N], F32, name="r_root")
         nc.scalar.activation(r_root[:], r[1][:], ABS_RSQRT)
-        r_size = held.tile([P, VB, widths[1]], F32, name="r_size")
+        nc.scalar.copy(reg_t[:], reg_t_ps[:])
+        r_size = held.tile([P, N], F32, name="r_size")
         nc.scalar.activation(r_size[:], r_root[:], SQUARE)
         nc.vector.tensor_tensor(q_bf[1][:], r_size[:], signed_words[:], MULT)
-        nc.scalar.copy(reg_t[:], reg_t_ps[:])
 
-        stores = [nc.scalar, nc.sync]
-        for k, (part, store) in enumerate(zip(parts, stores)):
-            u = psum.tile([C, widths[k]], F32, name=f"u{k}")
-            for b in range(VB):
-                nc.tensor.matmul(u[:], lhsT=reg_t[:, b, :], rhs=q_bf[k][:, b, :], start=(b == 0), stop=(b == VB - 1))
-            result = held.tile([C, widths[k]], F32, name=f"result{k}")
-            nc.vector.scalar_tensor_tensor(result[:], u[:], OLD_TO_NEW, theta[:, part], op0=ADD, op1=MULT)
-            nc.vector.tensor_scalar(result[:], result[:], RHO, -KEPT_ETA, op0=MULT, op1=ADD)
-            store.dma_start(out[:, part], result[:])
+        u = psum.tile([C, N], F32, name="u")
+        for b in range(VB):
+            nc.tensor.matmul(u[:], lhsT=reg_t[:, b, :], rhs=q_bf[b][:], start=(b == 0), stop=(b == VB - 1))
+        result = held.tile([C, N], F32, name="result")
+        nc.vector.scalar_tensor_tensor(result[:], u[:], OLD_TO_NEW, theta[:], op0=ADD, op1=MULT)
+        nc.vector.tensor_scalar(result[:], result[:], RHO, -KEPT_ETA, op0=MULT, op1=ADD)
+        nc.sync.dma_start(out, result[:])

@@ -26,12 +26,12 @@ def tile_mixehr_seed_kernel(tc, x, exp_n, bow, offs, out):
         tc.tile_pool(name="held", bufs=1) as held,
         tc.psum_pool(name="psum", bufs=1) as psum,
     ):
+        counts = held.tile([C, V], F32, name="counts")
+        nc.sync.dma_start(counts[:], exp_n)
         docs = held.tile([C, S], F32, name="docs")
-        nc.sync.dma_start(docs[:], x)
+        nc.scalar.dma_start(docs[:], x)
         offsets = held.tile([P, N // 16], U16, name="offsets")
         nc.sync.dma_start(offsets[:], offs)
-        counts = held.tile([C, V], F32, name="counts")
-        nc.scalar.dma_start(counts[:], exp_n)
         words = held.tile([P, VB, N], F32, name="words")
         nc.sync.dma_start(words[:], bow.rearrange("(b p) j -> p b j", p=P))
 

import concourse.mybir as mybir
from concourse.masks import make_identity

F32, BF16, U16 = mybir.dt.float32, mybir.dt.bfloat16, mybir.dt.uint16
ADD, MULT = mybir.AluOpType.add, mybir.AluOpType.mult
IDENTITY = mybir.ActivationFunctionType.Identity
SIGN = mybir.ActivationFunctionType.Sign
SQUARE = mybir.ActivationFunctionType.Square
ABS_RSQRT = mybir.ActivationFunctionType.Abs_reciprocal_sqrt

P = 128
C, V, S, N = 128, 256, 256, 128
VB = V // P
ETA = 0.1
BETA = 0.1
RHO = 8.0 ** (-0.9)
OLD_TO_NEW = (1.0 - RHO) / RHO
KEPT_ETA = (1.0 - RHO) * ETA

FLOPS = 2 * 2 * C * V * N


def tile_mixehr_seed_kernel(tc, x, exp_n, bow, offs, out):
    nc = tc.nc
    with (
        tc.tile_pool(name="held", bufs=1) as held,
        tc.psum_pool(name="psum", bufs=1) as psum,
    ):
        counts = held.tile([C, V], F32, name="counts")
        nc.sync.dma_start(counts[:], exp_n)
        docs = held.tile([C, S], F32, name="docs")
        nc.scalar.dma_start(docs[:], x)
        offsets = held.tile([P, N // 16], U16, name="offsets")
        nc.sync.dma_start(offsets[:], offs)
        words = held.tile([P, VB, N], F32, name="words")
        nc.sync.dma_start(words[:], bow.rearrange("(b p) j -> p b j", p=P))

        eta = held.tile([C, N], F32, name="eta")
        nc.gpsimd.memset(eta[:], ETA)
        beta = held.tile([C, 1], F32, name="beta")
        nc.gpsimd.memset(beta[:], BETA)
        warm = held.tile([C, 1], F32, name="warm")
        nc.scalar.activation(warm[:], beta[:], ABS_RSQRT)
        ident = held.tile([P, P], BF16, name="ident")
        make_identity(nc, ident[:])

        theta = held.tile([C, N], F32, name="theta")
        nc.vector.tensor_tensor(theta[:], docs[:].indirect(offsets[:]), eta[:], ADD)
        theta_bf = held.tile([C, N], BF16, name="theta_bf")
        nc.scalar.copy(theta_bf[:], theta[:])

        smoothed = held.tile([C, V], F32, name="smoothed")
        total = held.tile([C, 1], F32, name="total")
        nc.scalar.activation(smoothed[:], counts[:], IDENTITY, bias=beta[:, 0:1], accum_out=total[:])
        share = held.tile([C, 1], F32, name="share")
        nc.vector.reciprocal(share[:], total[:])
        reg_bf = [held.tile([C, P], BF16, name=f"reg_bf{b}") for b in range(VB)]
        for b in range(VB):
            nc.vector.tensor_scalar_mul(reg_bf[b][:], smoothed[:, b * P : (b + 1) * P], share[:, 0:1])

        r = [psum.tile([P, N], F32, name=f"r{b}") for b in range(VB)]
        for b in range(VB):
            nc.tensor.matmul(r[b][:], lhsT=reg_bf[b][:], rhs=theta_bf[:], start=True, stop=True)

        reg_t_ps = psum.tile([P, VB, C], BF16, name="reg_t_ps")
        for b in range(VB):
            nc.tensor.transpose(reg_t_ps[:, b, :], reg_bf[b][:], ident[:])
        reg_t = held.tile([P, VB, C], BF16, name="reg_t")

        q_bf = [held.tile([P, N], BF16, name=f"q_bf{b}") for b in range(VB)]
        r_inv = held.tile([P, N], F32, name="r_inv")
        nc.vector.reciprocal(r_inv[:], r[0][:])
        nc.vector.tensor_tensor(q_bf[0][:], r_inv[:], words[:, 0, :], MULT)
        r_sign = held.tile([P, N], F32, name="r_sign")
        nc.scalar.activation(r_sign[:], r[1][:], SIGN)
        signed_words = held.tile([P, N], F32, name="signed_words")
        nc.gpsimd.tensor_tensor(signed_words[:], r_sign[:], words[:, 1, :], MULT)
        r_root = held.tile([P, N], F32, name="r_root")
        nc.scalar.activation(r_root[:], r[1][:], ABS_RSQRT)
        nc.scalar.copy(reg_t[:], reg_t_ps[:])
        r_size = held.tile([P, N], F32, name="r_size")
        nc.scalar.activation(r_size[:], r_root[:], SQUARE)
        nc.vector.tensor_tensor(q_bf[1][:], r_size[:], signed_words[:], MULT)

        u = psum.tile([C, N], F32, name="u")
        for b in range(VB):
            nc.tensor.matmul(u[:], lhsT=reg_t[:, b, :], rhs=q_bf[b][:], start=(b == 0), stop=(b == VB - 1))
        result = held.tile([C, N], F32, name="result")
        nc.vector.scalar_tensor_tensor(result[:], u[:], OLD_TO_NEW, theta[:], op0=ADD, op1=MULT)
        nc.vector.tensor_scalar(result[:], result[:], RHO, -KEPT_ETA, op0=MULT, op1=ADD)
        nc.sync.dma_start(out, result[:])
